import numpy as np
import ml_dtypes


def mxq(x, axis, fmt="e4m3"):
    dtype, down = {"e4m3": (ml_dtypes.float8_e4m3fn, 7), "e5m2": (ml_dtypes.float8_e5m2, 14)}[fmt]
    v = np.moveaxis(np.asarray(x, np.float32).astype(ml_dtypes.bfloat16).astype(np.float64), axis, -1)
    blocks = v.reshape(v.shape[:-1] + (-1, 32))
    amax = np.abs(blocks).max(-1, keepdims=True)
    byte = np.maximum(np.where(amax > 0, np.frexp(amax)[1] - 1 + 127, 0) - down, 1)
    scale = np.exp2(byte - 127.0)
    codes = (blocks / scale).astype(np.float32).astype(dtype).astype(np.float64)
    return np.moveaxis((codes * scale).reshape(v.shape), -1, axis)


WIDE = False


def mx_kscale(k):
    if not WIDE:
        return np.ones(k)
    levels = np.array([10, -10, 5, -5, 0])
    a = np.random.permutation(np.resize(levels, k // 512 * 4)).reshape(k // 512, 4)
    idx = np.arange(k)
    return np.exp2(a[idx // 512, idx % 128 // 32])


BF16 = ml_dtypes.bfloat16


def bf(x):
    return np.asarray(x, np.float32).astype(BF16)


def f64(x):
    return np.asarray(x).astype(np.float64)


B, S, H, D = 16, 256, 2, 512
GAMMA = 64.0


def squash(v):
    return v / (1.0 + np.abs(v))


def setup_inputs():
    s = mx_kscale(D)
    return {"hq1": bf(np.random.standard_normal((B, H, S, D)) * 0.25 * s),
            "hk1": bf(np.random.standard_normal((B, H, S, D)) * 0.25 * s),
            "proj1": bf(np.random.standard_normal((1, H, D, D)) * 0.75 / np.sqrt(D) / s[:, None]),
            "bias1": bf(np.random.standard_normal((1, H, 1, D)) * 0.1)}


def reference(hq1, hk1, proj1, bias1):
    pq = mxq(f64(proj1), 2, "e4m3")
    hq = ((mxq(f64(hq1), 3, "e4m3") @ pq) + f64(bias1)) + f64(hq1)
    hk = ((mxq(f64(hk1), 3, "e4m3") @ pq) + f64(bias1)) + f64(hk1)
    qh = squash(hq * GAMMA)
    kh = squash(hk * GAMMA)
    return mxq(qh, 3, "e4m3") @ mxq(kh, 3, "e4m3").transpose(0, 1, 3, 2)

@@ -1,0 +1,233 @@
+from contextlib import ExitStack
+
+import concourse.mybir as mybir
+from concourse.masks import make_identity
+
+F32 = mybir.dt.float32
+BF16 = mybir.dt.bfloat16
+U32 = mybir.dt.uint32
+U8 = mybir.dt.uint8
+FP8X4 = mybir.dt.float8_e4m3fn_x4
+ACT = mybir.ActivationFunctionType
+ALU = mybir.AluOpType
+
+P = 128
+PACK = 4
+B, H, S, D = 16, 2, 256, 512
+PAIRS = B * H
+TOK = 2 * S
+WORDS = D // 2
+GAMMA = 64.0
+LOAD_AHEAD = 2
+
+FLOPS = 2 * PAIRS * (TOK * D * D + S * S * D)
+
+
+def tile_decoder_pb_t_kernel(tc, hq1, hk1, proj1, bias1, out):
+    nc = tc.nc
+    with ExitStack() as ctx:
+        ctx.enter_context(tc.manual_schedule())
+        keep = ctx.enter_context(tc.tile_pool(name="keep", bufs=1))
+        setup = ctx.enter_context(tc.tile_pool(name="setup", bufs=2))
+        loads = ctx.enter_context(tc.tile_pool(name="loads", bufs=4))
+        work = ctx.enter_context(tc.tile_pool(name="work", bufs=2))
+        sums = ctx.enter_context(tc.tile_pool(name="sums", bufs=3))
+        psum_t = ctx.enter_context(tc.psum_pool(name="psum_t", bufs=2))
+        psum_a = ctx.enter_context(tc.psum_pool(name="psum_a", bufs=4))
+        psum_o = ctx.enter_context(tc.psum_pool(name="psum_o", bufs=2))
+
+        tiles = {}
+
+        ident = keep.tile([P, P], F32)
+        make_identity(nc, ident[:])
+        one = keep.tile([P, 1], F32)
+        nc.vector.memset(one[:], 1.0)
+
+        bias = keep.tile([P, H * PACK], BF16)
+
+        def load_bias():
+            nc.sync.dma_start(
+                out=bias[:].rearrange("p (a e) -> p a e", e=2),
+                in_=bias1.rearrange("o h i (u p e) -> p (o h i u) e", u=2, e=2),
+            )
+
+        w_codes = keep.tile([P, H, D], U32, align_bytes=64)
+        w_scales = keep.tile([P, H, D], U8, align_bytes=64)
+
+        def load_weights(h):
+            rows = setup.tile([P, PACK, D], BF16)
+            nc.sync.dma_start(
+                out=rows[:].rearrange("p (u e) n -> p u (e n)", e=2),
+                in_=proj1[0, h].rearrange("(u p e) n -> p u (e n)", u=2, e=2),
+            )
+            tiles["rows", h] = rows
+
+        def quantise_weights(h):
+            by_chunk = tiles["rows", h][:].rearrange("p t (u m e) -> p u e m t", u=2, e=2)
+            w_words = setup.tile([P, PACK, P, PACK], BF16, align_bytes=64)
+            for c in range(PACK):
+                nc.vector.tensor_copy(out=w_words[:, c, :, :], in_=by_chunk[:, c // 2, c % 2, :, :])
+            nc.vector.quantize_mx(
+                out=w_codes[:, h, :].bitcast(FP8X4),
+                scales=w_scales[:, h, :],
+                in_=w_words[:].rearrange("p c m t -> p (c m t)"),
+            )
+
+        def load(i):
+            b, h = divmod(i, H)
+            x = loads.tile([P, 2, S // P, D], BF16)
+            for side, src in enumerate((hq1, hk1)):
+                nc.sync.dma_start(
+                    out=x[:, side, :, :], in_=src[b, h].rearrange("(j p) d -> p j d", p=P)
+                )
+            tiles["x", i] = x
+
+        def transpose(i):
+            words = tiles["x", i][:].rearrange("p a j d -> p (a j d)").bitcast(F32)
+            for side in range(2):
+                xt = psum_t.tile([P, 2, S], F32)
+                for j in range(S // P):
+                    for u in range(2):
+                        first = (side * (S // P) + j) * WORDS + u * P
+                        nc.tensor.transpose(
+                            xt[:, u, j * P : (j + 1) * P], words[:, first : first + P], ident[:]
+                        )
+                tiles["xt", i, side] = xt
+
+        def regroup(i):
+            x_t = work.tile([P, TOK * PACK], BF16, align_bytes=64)
+            by_token = x_t[:].bitcast(F32).rearrange("p (s u) -> p s u", u=2)
+            for side in range(2):
+                nc.vector.tensor_copy(
+                    out=by_token[:, side * S : (side + 1) * S, :],
+                    in_=tiles["xt", i, side][:].rearrange("p u s -> p s u"),
+                )
+            tiles["x_t", i] = x_t
+
+        def quantise_input(i):
+            x_codes = work.tile([P, TOK], U32, align_bytes=64)
+            x_scales = work.tile([P, TOK], U8, align_bytes=64)
+            nc.vector.quantize_mx(
+                out=x_codes[:].bitcast(FP8X4), scales=x_scales[:], in_=tiles["x_t", i][:]
+            )
+            tiles["x_mx", i] = (x_codes, x_scales)
+
+        def project(i):
+            h = i % H
+            x_codes, x_scales = tiles["x_mx", i]
+            residual = tiles["x_t", i][:].rearrange("p (s t) -> p s t", t=PACK)
+            z = sums.tile([P, PACK, TOK], F32)
+            for c in range(PACK):
+                cols = slice(c * P, (c + 1) * P)
+                acc = psum_a.tile([P, TOK], F32)
+                nc.tensor.matmul_mx(
+                    out=acc[:],
+                    lhsT=w_codes[:, h, cols].bitcast(FP8X4),
+                    lhsT_scale=w_scales[:, h, cols],
+                    rhs=x_codes[:].bitcast(FP8X4),
+                    rhs_scale=x_scales[:],
+                    start=True,
+                    stop=True,
+                )
+                nc.vector.scalar_tensor_tensor(
+                    out=z[:, c, :],
+                    in0=acc[:],
+                    scalar=bias[:, h * PACK + c : h * PACK + c + 1],
+                    in1=residual[:, :, c],
+                    op0=ALU.add,
+                    op1=ALU.add,
+                )
+            tiles["z", i] = z
+
+        def squash_factor(i):
+            z = tiles["z", i]
+            r = work.tile([P, TOK * PACK], F32)
+            sides = range(2)
+            mags, roots = [], []
+            for side in sides:
+                mag = work.tile([P, 2, S, 2], F32)
+                nc.scalar.activation(
+                    out=mag[:],
+                    in_=z[:, :, side * S : (side + 1) * S].rearrange("p (u e) s -> p u s e", e=2),
+                    func=ACT.Abs,
+                )
+                mags.append(mag)
+            for side in sides:
+                root = work.tile([P, S, 2, 2], F32)
+                nc.scalar.activation(
+                    out=root[:],
+                    in_=mags[side][:].rearrange("p u s e -> p s u e"),
+                    func=ACT.Abs_reciprocal_sqrt,
+                    scale=GAMMA,
+                    bias=one[:, 0:1],
+                )
+                roots.append(root)
+            for side in sides:
+                nc.scalar.activation(
+                    out=r[:, side * S * PACK : (side + 1) * S * PACK],
+                    in_=roots[side][:].rearrange("p s u e -> p (s u e)"),
+                    func=ACT.Square,
+                    scale=GAMMA**0.5,
+                )
+            tiles["r", i] = r
+
+        def squash_apply(i):
+            y = work.tile([P, TOK * PACK], BF16, align_bytes=64)
+            nc.vector.tensor_tensor(
+                out=y[:].rearrange("p (s t) -> p s t", t=PACK),
+                in0=tiles["z", i][:].rearrange("p t s -> p s t"),
+                in1=tiles["r", i][:].rearrange("p (s t) -> p s t", t=PACK),
+                op=ALU.mult,
+            )
+            tiles["y", i] = y
+
+        def quantise_hash(i):
+            y_codes = work.tile([P, TOK], U32, align_bytes=64)
+            y_scales = work.tile([P, TOK], U8, align_bytes=64)
+            nc.vector.quantize_mx(
+                out=y_codes[:].bitcast(FP8X4), scales=y_scales[:], in_=tiles["y", i][:]
+            )
+            tiles["y_mx", i] = (y_codes, y_scales)
+
+        def scores(i):
+            b, h = divmod(i, H)
+            y_codes, y_scales = tiles["y_mx", i]
+            keys = slice(S, TOK)
+            prod = psum_o.tile([P, S // P, S], F32)
+            for j in range(S // P):
+                queries = slice(j * P, (j + 1) * P)
+                nc.tensor.matmul_mx(
+                    out=prod[:, j, :],
+                    lhsT=y_codes[:, queries].bitcast(FP8X4),
+                    lhsT_scale=y_scales[:, queries],
+                    rhs=y_codes[:, keys].bitcast(FP8X4),
+                    rhs_scale=y_scales[:, keys],
+                    start=True,
+                    stop=True,
+                )
+            result = work.tile([P, S // P, S], F32)
+            nc.scalar.copy(out=result[:], in_=prod[:])
+            nc.sync.dma_start(out=out[b, h].rearrange("(j m) k -> m j k", m=P), in_=result[:])
+
+        def each(stage, i):
+            if 0 <= i < PAIRS:
+                stage(i)
+
+        load_weights(0)
+        for i in range(LOAD_AHEAD):
+            load(i)
+        load_bias()
+        load_weights(1)
+        for k in range(-2, PAIRS + 1):
+            ahead = k + 2
+            each(load, ahead + LOAD_AHEAD)
+            each(transpose, ahead)
+            each(squash_factor, k)
+            each(quantise_input, k + 1)
+            each(squash_apply, k - 1)
+            each(project, k + 1)
+            each(quantise_hash, k - 1)
+            each(scores, k - 1)
+            if ahead < H:
+                quantise_weights(ahead)
+            each(regroup, ahead)

@@ -173,12 +173,14 @@ def tile_decoder_pb_t_kernel(tc, hq1, hk1, proj1, bias1, out):
 
         def squash_apply(i):
             y = work.tile([P, TOK * PACK], BF16, align_bytes=64)
-            nc.vector.tensor_tensor(
-                out=y[:].rearrange("p (s t) -> p s t", t=PACK),
-                in0=tiles["z", i][:].rearrange("p t s -> p s t"),
-                in1=tiles["r", i][:].rearrange("p (s t) -> p s t", t=PACK),
-                op=ALU.mult,
-            )
+            for side in range(2):
+                tokens = slice(side * S, (side + 1) * S)
+                nc.gpsimd.tensor_tensor(
+                    out=y[:].rearrange("p (s t) -> p s t", t=PACK)[:, tokens, :],
+                    in0=tiles["z", i][:, :, tokens].rearrange("p t s -> p s t"),
+                    in1=tiles["r", i][:].rearrange("p (s t) -> p s t", t=PACK)[:, tokens, :],
+                    op=ALU.mult,
+                )
             tiles["y", i] = y
 
         def quantise_hash(i):
@@ -190,7 +192,6 @@ def tile_decoder_pb_t_kernel(tc, hq1, hk1, proj1, bias1, out):
             tiles["y_mx", i] = (y_codes, y_scales)
 
         def scores(i):
-            b, h = divmod(i, H)
             y_codes, y_scales = tiles["y_mx", i]
             keys = slice(S, TOK)
             prod = psum_o.tile([P, S // P, S], F32)
@@ -205,8 +206,12 @@ def tile_decoder_pb_t_kernel(tc, hq1, hk1, proj1, bias1, out):
                     start=True,
                     stop=True,
                 )
+            tiles["prod", i] = prod
+
+        def store(i):
+            b, h = divmod(i, H)
             result = work.tile([P, S // P, S], F32)
-            nc.scalar.copy(out=result[:], in_=prod[:])
+            nc.vector.tensor_copy(out=result[:], in_=tiles["prod", i][:])
             nc.sync.dma_start(out=out[b, h].rearrange("(j m) k -> m j k", m=P), in_=result[:])
 
         def each(stage, i):
@@ -218,16 +223,16 @@ def tile_decoder_pb_t_kernel(tc, hq1, hk1, proj1, bias1, out):
             load(i)
         load_bias()
         load_weights(1)
-        for k in range(-2, PAIRS + 1):
-            ahead = k + 2
-            each(load, ahead + LOAD_AHEAD)
-            each(transpose, ahead)
+        for k in range(-3, PAIRS + 2):
+            each(load, k + 3 + LOAD_AHEAD)
             each(squash_factor, k)
-            each(quantise_input, k + 1)
             each(squash_apply, k - 1)
             each(project, k + 1)
+            if 0 <= k + 2 < H:
+                quantise_weights(k + 2)
+            each(regroup, k + 2)
+            each(transpose, k + 3)
+            each(store, k - 2)
             each(quantise_hash, k - 1)
             each(scores, k - 1)
-            if ahead < H:
-                quantise_weights(ahead)
-            each(regroup, ahead)
+            each(quantise_input, k + 2)

@@ -141,33 +141,26 @@ def tile_decoder_pb_t_kernel(tc, hq1, hk1, proj1, bias1, out):
 
         def squash_factor(i):
             z = tiles["z", i]
-            r = work.tile([P, TOK * PACK], F32)
-            sides = range(2)
+            r = work.tile([P, PACK, TOK], F32)
+            sides = [slice(side * S, (side + 1) * S) for side in range(2)]
             mags, roots = [], []
-            for side in sides:
-                mag = work.tile([P, 2, S, 2], F32)
-                nc.scalar.activation(
-                    out=mag[:],
-                    in_=z[:, :, side * S : (side + 1) * S].rearrange("p (u e) s -> p u s e", e=2),
-                    func=ACT.Abs,
-                )
+            for tokens in sides:
+                mag = work.tile([P, PACK, S], F32)
+                nc.scalar.activation(out=mag[:], in_=z[:, :, tokens], func=ACT.Abs)
                 mags.append(mag)
-            for side in sides:
-                root = work.tile([P, S, 2, 2], F32)
+            for mag in mags:
+                root = work.tile([P, PACK, S], F32)
                 nc.scalar.activation(
                     out=root[:],
-                    in_=mags[side][:].rearrange("p u s e -> p s u e"),
+                    in_=mag[:],
                     func=ACT.Abs_reciprocal_sqrt,
                     scale=GAMMA,
                     bias=one[:, 0:1],
                 )
                 roots.append(root)
-            for side in sides:
+            for tokens, root in zip(sides, roots):
                 nc.scalar.activation(
-                    out=r[:, side * S * PACK : (side + 1) * S * PACK],
-                    in_=roots[side][:].rearrange("p s u e -> p (s u e)"),
-                    func=ACT.Square,
-                    scale=GAMMA**0.5,
+                    out=r[:, :, tokens], in_=root[:], func=ACT.Square, scale=GAMMA**0.5
                 )
             tiles["r", i] = r
 
@@ -178,7 +171,7 @@ def tile_decoder_pb_t_kernel(tc, hq1, hk1, proj1, bias1, out):
                 nc.gpsimd.tensor_tensor(
                     out=y[:].rearrange("p (s t) -> p s t", t=PACK)[:, tokens, :],
                     in0=tiles["z", i][:, :, tokens].rearrange("p t s -> p s t"),
-                    in1=tiles["r", i][:].rearrange("p (s t) -> p s t", t=PACK)[:, tokens, :],
+                    in1=tiles["r", i][:, :, tokens].rearrange("p t s -> p s t"),
                     op=ALU.mult,
                 )
             tiles["y", i] = y

@@ -18,6 +18,7 @@ PAIRS = B * H
 TOK = 2 * S
 WORDS = D // 2
 GAMMA = 64.0
+RUN = 4
 LOAD_AHEAD = 2
 
 FLOPS = 2 * PAIRS * (TOK * D * D + S * S * D)
@@ -166,12 +167,13 @@ def tile_decoder_pb_t_kernel(tc, hq1, hk1, proj1, bias1, out):
 
         def squash_apply(i):
             y = work.tile([P, TOK * PACK], BF16, align_bytes=64)
+            by_token = y[:].rearrange("p (s t) -> p s t", t=PACK)
             for side in range(2):
                 tokens = slice(side * S, (side + 1) * S)
                 nc.gpsimd.tensor_tensor(
-                    out=y[:].rearrange("p (s t) -> p s t", t=PACK)[:, tokens, :],
-                    in0=tiles["z", i][:, :, tokens].rearrange("p t s -> p s t"),
-                    in1=tiles["r", i][:, :, tokens].rearrange("p t s -> p s t"),
+                    out=by_token[:, tokens, :].rearrange("p (n i) t -> p n t i", i=RUN),
+                    in0=tiles["z", i][:, :, tokens].rearrange("p t (n i) -> p n t i", i=RUN),
+                    in1=tiles["r", i][:, :, tokens].rearrange("p t (n i) -> p n t i", i=RUN),
                     op=ALU.mult,
                 )
             tiles["y", i] = y

@@ -19,6 +19,7 @@ TOK = 2 * S
 WORDS = D // 2
 GAMMA = 64.0
 RUN = 4
+SHARE = 128
 LOAD_AHEAD = 2
 
 FLOPS = 2 * PAIRS * (TOK * D * D + S * S * D)
@@ -67,7 +68,7 @@ def tile_decoder_pb_t_kernel(tc, hq1, hk1, proj1, bias1, out):
             by_chunk = tiles["rows", h][:].rearrange("p t (u m e) -> p u e m t", u=2, e=2)
             w_words = setup.tile([P, PACK, P, PACK], BF16, align_bytes=64)
             for c in range(PACK):
-                nc.vector.tensor_copy(out=w_words[:, c, :, :], in_=by_chunk[:, c // 2, c % 2, :, :])
+                nc.scalar.copy(out=w_words[:, c, :, :], in_=by_chunk[:, c // 2, c % 2, :, :])
             nc.vector.quantize_mx(
                 out=w_codes[:, h, :].bitcast(FP8X4),
                 scales=w_scales[:, h, :],
@@ -116,8 +117,6 @@ def tile_decoder_pb_t_kernel(tc, hq1, hk1, proj1, bias1, out):
         def project(i):
             h = i % H
             x_codes, x_scales = tiles["x_mx", i]
-            residual = tiles["x_t", i][:].rearrange("p (s t) -> p s t", t=PACK)
-            z = sums.tile([P, PACK, TOK], F32)
             for c in range(PACK):
                 cols = slice(c * P, (c + 1) * P)
                 acc = psum_a.tile([P, TOK], F32)
@@ -130,9 +129,16 @@ def tile_decoder_pb_t_kernel(tc, hq1, hk1, proj1, bias1, out):
                     start=True,
                     stop=True,
                 )
+                tiles["acc", i, c] = acc
+
+        def add_residual(i):
+            h = i % H
+            residual = tiles["x_t", i][:].rearrange("p (s t) -> p s t", t=PACK)
+            z = sums.tile([P, PACK, TOK], F32)
+            for c in range(PACK):
                 nc.vector.scalar_tensor_tensor(
                     out=z[:, c, :],
-                    in0=acc[:],
+                    in0=tiles["acc", i, c][:],
                     scalar=bias[:, h * PACK + c : h * PACK + c + 1],
                     in1=residual[:, :, c],
                     op0=ALU.add,
@@ -140,16 +146,30 @@ def tile_decoder_pb_t_kernel(tc, hq1, hk1, proj1, bias1, out):
                 )
             tiles["z", i] = z
 
+        def magnitude_share(i):
+            mag_keys = work.tile([P, PACK, S], F32)
+            z_share = tiles["z", i][:, :, TOK - SHARE :]
+            nc.vector.scalar_tensor_tensor(
+                out=mag_keys[:, :, S - SHARE :],
+                in0=z_share,
+                scalar=-1.0,
+                in1=z_share,
+                op0=ALU.mult,
+                op1=ALU.max,
+            )
+            tiles["mag_keys", i] = mag_keys
+
         def squash_factor(i):
             z = tiles["z", i]
             r = work.tile([P, PACK, TOK], F32)
-            sides = [slice(side * S, (side + 1) * S) for side in range(2)]
-            mags, roots = [], []
-            for tokens in sides:
-                mag = work.tile([P, PACK, S], F32)
-                nc.scalar.activation(out=mag[:], in_=z[:, :, tokens], func=ACT.Abs)
-                mags.append(mag)
-            for mag in mags:
+            mag_queries = work.tile([P, PACK, S], F32)
+            mag_keys = tiles["mag_keys", i]
+            nc.scalar.activation(out=mag_queries[:], in_=z[:, :, :S], func=ACT.Abs)
+            nc.scalar.activation(
+                out=mag_keys[:, :, : S - SHARE], in_=z[:, :, S : TOK - SHARE], func=ACT.Abs
+            )
+            roots = []
+            for mag in (mag_queries, mag_keys):
                 root = work.tile([P, PACK, S], F32)
                 nc.scalar.activation(
                     out=root[:],
@@ -159,24 +179,32 @@ def tile_decoder_pb_t_kernel(tc, hq1, hk1, proj1, bias1, out):
                     bias=one[:, 0:1],
                 )
                 roots.append(root)
-            for tokens, root in zip(sides, roots):
+            for side, root in enumerate(roots):
                 nc.scalar.activation(
-                    out=r[:, :, tokens], in_=root[:], func=ACT.Square, scale=GAMMA**0.5
+                    out=r[:, :, side * S : (side + 1) * S],
+                    in_=root[:],
+                    func=ACT.Square,
+                    scale=GAMMA**0.5,
                 )
             tiles["r", i] = r
 
+        def multiply(engine, i, tokens):
+            by_token = tiles["y", i][:].rearrange("p (s t) -> p s t", t=PACK)
+            engine.tensor_tensor(
+                out=by_token[:, tokens, :].rearrange("p (n i) t -> p n t i", i=RUN),
+                in0=tiles["z", i][:, :, tokens].rearrange("p t (n i) -> p n t i", i=RUN),
+                in1=tiles["r", i][:, :, tokens].rearrange("p t (n i) -> p n t i", i=RUN),
+                op=ALU.mult,
+            )
+
         def squash_apply(i):
             y = work.tile([P, TOK * PACK], BF16, align_bytes=64)
-            by_token = y[:].rearrange("p (s t) -> p s t", t=PACK)
-            for side in range(2):
-                tokens = slice(side * S, (side + 1) * S)
-                nc.gpsimd.tensor_tensor(
-                    out=by_token[:, tokens, :].rearrange("p (n i) t -> p n t i", i=RUN),
-                    in0=tiles["z", i][:, :, tokens].rearrange("p t (n i) -> p n t i", i=RUN),
-                    in1=tiles["r", i][:, :, tokens].rearrange("p t (n i) -> p n t i", i=RUN),
-                    op=ALU.mult,
-                )
             tiles["y", i] = y
+            multiply(nc.gpsimd, i, slice(S, TOK - SHARE))
+            multiply(nc.gpsimd, i, slice(0, S))
+
+        def squash_apply_share(i):
+            multiply(nc.vector, i, slice(TOK - SHARE, TOK))
 
         def quantise_hash(i):
             y_codes = work.tile([P, TOK], U32, align_bytes=64)
@@ -222,12 +250,15 @@ def tile_decoder_pb_t_kernel(tc, hq1, hk1, proj1, bias1, out):
             each(load, k + 3 + LOAD_AHEAD)
             each(squash_factor, k)
             each(squash_apply, k - 1)
-            each(project, k + 1)
-            if 0 <= k + 2 < H:
-                quantise_weights(k + 2)
             each(regroup, k + 2)
             each(transpose, k + 3)
+            each(add_residual, k + 1)
             each(store, k - 2)
+            each(magnitude_share, k + 1)
+            each(squash_apply_share, k - 1)
+            if 0 <= k + 2 < H:
+                quantise_weights(k + 2)
+            each(quantise_input, k + 2)
+            each(project, k + 2)
             each(quantise_hash, k - 1)
             each(scores, k - 1)
-            each(quantise_input, k + 2)

@@ -19,7 +19,8 @@ TOK = 2 * S
 WORDS = D // 2
 GAMMA = 64.0
 RUN = 4
-SHARE = 128
+ABS_SHARE = 96
+MUL_SHARE = 160
 LOAD_AHEAD = 2
 
 FLOPS = 2 * PAIRS * (TOK * D * D + S * S * D)
@@ -148,9 +149,9 @@ def tile_decoder_pb_t_kernel(tc, hq1, hk1, proj1, bias1, out):
 
         def magnitude_share(i):
             mag_keys = work.tile([P, PACK, S], F32)
-            z_share = tiles["z", i][:, :, TOK - SHARE :]
+            z_share = tiles["z", i][:, :, TOK - ABS_SHARE :]
             nc.vector.scalar_tensor_tensor(
-                out=mag_keys[:, :, S - SHARE :],
+                out=mag_keys[:, :, S - ABS_SHARE :],
                 in0=z_share,
                 scalar=-1.0,
                 in1=z_share,
@@ -166,7 +167,7 @@ def tile_decoder_pb_t_kernel(tc, hq1, hk1, proj1, bias1, out):
             mag_keys = tiles["mag_keys", i]
             nc.scalar.activation(out=mag_queries[:], in_=z[:, :, :S], func=ACT.Abs)
             nc.scalar.activation(
-                out=mag_keys[:, :, : S - SHARE], in_=z[:, :, S : TOK - SHARE], func=ACT.Abs
+                out=mag_keys[:, :, : S - ABS_SHARE], in_=z[:, :, S : TOK - ABS_SHARE], func=ACT.Abs
             )
             roots = []
             for mag in (mag_queries, mag_keys):
@@ -200,11 +201,11 @@ def tile_decoder_pb_t_kernel(tc, hq1, hk1, proj1, bias1, out):
         def squash_apply(i):
             y = work.tile([P, TOK * PACK], BF16, align_bytes=64)
             tiles["y", i] = y
-            multiply(nc.gpsimd, i, slice(S, TOK - SHARE))
+            multiply(nc.gpsimd, i, slice(S, TOK - MUL_SHARE))
             multiply(nc.gpsimd, i, slice(0, S))
 
         def squash_apply_share(i):
-            multiply(nc.vector, i, slice(TOK - SHARE, TOK))
+            multiply(nc.vector, i, slice(TOK - MUL_SHARE, TOK))
 
         def quantise_hash(i):
             y_codes = work.tile([P, TOK], U32, align_bytes=64)

@@ -20,7 +20,7 @@ WORDS = D // 2
 GAMMA = 64.0
 RUN = 4
 ABS_SHARE = 96
-MUL_SHARE = 160
+MUL_SHARE = 96
 LOAD_AHEAD = 2
 
 FLOPS = 2 * PAIRS * (TOK * D * D + S * S * D)

@@ -23,6 +23,9 @@ ABS_SHARE = 96
 MUL_SHARE = 96
 LOAD_AHEAD = 2
 
+BY_CHUNK = 2
+LAST = PAIRS - 1
+
 FLOPS = 2 * PAIRS * (TOK * D * D + S * S * D)
 
 
@@ -45,6 +48,8 @@ def tile_decoder_pb_t_kernel(tc, hq1, hk1, proj1, bias1, out):
         make_identity(nc, ident[:])
         one = keep.tile([P, 1], F32)
         nc.vector.memset(one[:], 1.0)
+        warm = keep.tile([P, 1], F32)
+        nc.scalar.activation(out=warm[:], in_=one[:], func=ACT.Abs_reciprocal_sqrt)
 
         bias = keep.tile([P, H * PACK], BF16)
 
@@ -65,19 +70,34 @@ def tile_decoder_pb_t_kernel(tc, hq1, hk1, proj1, bias1, out):
             )
             tiles["rows", h] = rows
 
-        def quantise_weights(h):
+        def order_weights(h):
             by_chunk = tiles["rows", h][:].rearrange("p t (u m e) -> p u e m t", u=2, e=2)
             w_words = setup.tile([P, PACK, P, PACK], BF16, align_bytes=64)
             for c in range(PACK):
-                nc.scalar.copy(out=w_words[:, c, :, :], in_=by_chunk[:, c // 2, c % 2, :, :])
+                chunk = by_chunk[:, c // 2, c % 2, :, :]
+                if h == 1:
+                    nc.gpsimd.tensor_scalar(
+                        out=w_words[:, c, :, :],
+                        in0=chunk,
+                        scalar1=1.0,
+                        scalar2=0.0,
+                        op0=ALU.mult,
+                        op1=ALU.add,
+                    )
+                else:
+                    copy = nc.scalar.copy if c < PACK // 2 else nc.vector.tensor_copy
+                    copy(out=w_words[:, c, :, :], in_=chunk)
+            tiles["w_words", h] = w_words
+
+        def quantise_weights(h):
             nc.vector.quantize_mx(
                 out=w_codes[:, h, :].bitcast(FP8X4),
                 scales=w_scales[:, h, :],
-                in_=w_words[:].rearrange("p c m t -> p (c m t)"),
+                in_=tiles["w_words", h][:].rearrange("p c m t -> p (c m t)"),
             )
 
         def load(i):
-            b, h = divmod(i, H)
+            h, b = divmod(i, B)
             x = loads.tile([P, 2, S // P, D], BF16)
             for side, src in enumerate((hq1, hk1)):
                 nc.sync.dma_start(
@@ -116,7 +136,7 @@ def tile_decoder_pb_t_kernel(tc, hq1, hk1, proj1, bias1, out):
             tiles["x_mx", i] = (x_codes, x_scales)
 
         def project(i):
-            h = i % H
+            h = i // B
             x_codes, x_scales = tiles["x_mx", i]
             for c in range(PACK):
                 cols = slice(c * P, (c + 1) * P)
@@ -133,7 +153,7 @@ def tile_decoder_pb_t_kernel(tc, hq1, hk1, proj1, bias1, out):
                 tiles["acc", i, c] = acc
 
         def add_residual(i):
-            h = i % H
+            h = i // B
             residual = tiles["x_t", i][:].rearrange("p (s t) -> p s t", t=PACK)
             z = sums.tile([P, PACK, TOK], F32)
             for c in range(PACK):
@@ -149,26 +169,36 @@ def tile_decoder_pb_t_kernel(tc, hq1, hk1, proj1, bias1, out):
 
         def magnitude_share(i):
             mag_keys = work.tile([P, PACK, S], F32)
-            z_share = tiles["z", i][:, :, TOK - ABS_SHARE :]
+            tiles["mag_keys", i] = mag_keys
+            if i < BY_CHUNK:
+                return
+            share = S if i == LAST else ABS_SHARE
+            z_share = tiles["z", i][:, :, TOK - share :]
             nc.vector.scalar_tensor_tensor(
-                out=mag_keys[:, :, S - ABS_SHARE :],
+                out=mag_keys[:, :, S - share :],
                 in0=z_share,
                 scalar=-1.0,
                 in1=z_share,
                 op0=ALU.mult,
                 op1=ALU.max,
             )
-            tiles["mag_keys", i] = mag_keys
 
         def squash_factor(i):
             z = tiles["z", i]
             r = work.tile([P, PACK, TOK], F32)
             mag_queries = work.tile([P, PACK, S], F32)
             mag_keys = tiles["mag_keys", i]
-            nc.scalar.activation(out=mag_queries[:], in_=z[:, :, :S], func=ACT.Abs)
-            nc.scalar.activation(
-                out=mag_keys[:, :, : S - ABS_SHARE], in_=z[:, :, S : TOK - ABS_SHARE], func=ACT.Abs
-            )
+            if i < BY_CHUNK:
+                for c in range(PACK):
+                    nc.scalar.activation(out=mag_queries[:, c, :], in_=z[:, c, :S], func=ACT.Abs)
+                    nc.scalar.activation(out=mag_keys[:, c, :], in_=z[:, c, S:], func=ACT.Abs)
+            else:
+                nc.scalar.activation(out=mag_queries[:], in_=z[:, :, :S], func=ACT.Abs)
+                nc.scalar.activation(
+                    out=mag_keys[:, :, : S - ABS_SHARE],
+                    in_=z[:, :, S : TOK - ABS_SHARE],
+                    func=ACT.Abs,
+                )
             roots = []
             for mag in (mag_queries, mag_keys):
                 root = work.tile([P, PACK, S], F32)
@@ -189,6 +219,30 @@ def tile_decoder_pb_t_kernel(tc, hq1, hk1, proj1, bias1, out):
                 )
             tiles["r", i] = r
 
+        def squash_factor_last(i):
+            r = work.tile([P, PACK, TOK], F32)
+            mag_queries = work.tile([P, PACK, S], F32)
+            mag_keys = tiles["mag_keys", i]
+            root_q = work.tile([P, PACK, S], F32, tag="root")
+            root_k = work.tile([P, PACK, S], F32, tag="root")
+
+            def root(out, in_):
+                nc.scalar.activation(
+                    out=out, in_=in_, func=ACT.Abs_reciprocal_sqrt, scale=GAMMA, bias=one[:, 0:1]
+                )
+
+            def factor(out, in_):
+                nc.scalar.activation(out=out, in_=in_, func=ACT.Square, scale=GAMMA**0.5)
+
+            nc.scalar.activation(out=mag_queries[:], in_=tiles["z", i][:, :, :S], func=ACT.Abs)
+            root(root_k[:], mag_keys[:])
+            root(root_q[:, :, :P], mag_queries[:, :, :P])
+            factor(r[:, :, S:], root_k[:])
+            root(root_q[:, :, P:], mag_queries[:, :, P:])
+            factor(r[:, :, :P], root_q[:, :, :P])
+            factor(r[:, :, P:S], root_q[:, :, P:])
+            tiles["r", i] = r
+
         def multiply(engine, i, tokens):
             by_token = tiles["y", i][:].rearrange("p (s t) -> p s t", t=PACK)
             engine.tensor_tensor(
@@ -201,11 +255,13 @@ def tile_decoder_pb_t_kernel(tc, hq1, hk1, proj1, bias1, out):
         def squash_apply(i):
             y = work.tile([P, TOK * PACK], BF16, align_bytes=64)
             tiles["y", i] = y
+            if i >= LAST - 1:
+                return
             multiply(nc.gpsimd, i, slice(S, TOK - MUL_SHARE))
             multiply(nc.gpsimd, i, slice(0, S))
 
         def squash_apply_share(i):
-            multiply(nc.vector, i, slice(TOK - MUL_SHARE, TOK))
+            multiply(nc.vector, i, slice(TOK - MUL_SHARE if i < LAST - 1 else 0, TOK))
 
         def quantise_hash(i):
             y_codes = work.tile([P, TOK], U32, align_bytes=64)
@@ -214,6 +270,43 @@ def tile_decoder_pb_t_kernel(tc, hq1, hk1, proj1, bias1, out):
                 out=y_codes[:].bitcast(FP8X4), scales=y_scales[:], in_=tiles["y", i][:]
             )
             tiles["y_mx", i] = (y_codes, y_scales)
+
+        def finish(i):
+            h, b = divmod(i, B)
+            y = work.tile([P, TOK * PACK], BF16, align_bytes=64)
+            tiles["y", i] = y
+            y_codes = work.tile([P, TOK], U32, align_bytes=64)
+            y_scales = work.tile([P, TOK], U8, align_bytes=64)
+            keys, halves = slice(S, TOK), (slice(0, P), slice(P, S))
+
+            def quantise(tokens):
+                nc.vector.quantize_mx(
+                    out=y_codes[:, tokens].bitcast(FP8X4),
+                    scales=y_scales[:, tokens],
+                    in_=y[:, tokens.start * PACK : tokens.stop * PACK],
+                )
+
+            multiply(nc.vector, i, keys)
+            multiply(nc.vector, i, halves[0])
+            quantise(keys)
+            quantise(halves[0])
+            multiply(nc.vector, i, halves[1])
+            quantise(halves[1])
+            for j, queries in enumerate(halves):
+                acc = psum_a.tile([P, TOK], F32)
+                nc.tensor.matmul_mx(
+                    out=acc[:, :S],
+                    lhsT=y_codes[:, queries].bitcast(FP8X4),
+                    lhsT_scale=y_scales[:, queries],
+                    rhs=y_codes[:, keys].bitcast(FP8X4),
+                    rhs_scale=y_scales[:, keys],
+                    start=True,
+                    stop=True,
+                )
+                half = work.tile([P, S], F32)
+                copy = nc.scalar.copy if j == 0 else nc.vector.tensor_copy
+                copy(out=half[:], in_=acc[:, :S])
+                nc.sync.dma_start(out=out[b, h, queries, :], in_=half[:])
 
         def scores(i):
             y_codes, y_scales = tiles["y_mx", i]
@@ -233,23 +326,41 @@ def tile_decoder_pb_t_kernel(tc, hq1, hk1, proj1, bias1, out):
             tiles["prod", i] = prod
 
         def store(i):
-            b, h = divmod(i, H)
+            h, b = divmod(i, B)
             result = work.tile([P, S // P, S], F32)
-            nc.vector.tensor_copy(out=result[:], in_=tiles["prod", i][:])
+            copy = nc.vector.tensor_copy if i < LAST - 2 else nc.scalar.copy
+            copy(out=result[:], in_=tiles["prod", i][:])
             nc.sync.dma_start(out=out[b, h].rearrange("(j m) k -> m j k", m=P), in_=result[:])
 
         def each(stage, i):
             if 0 <= i < PAIRS:
                 stage(i)
 
+        load(0)
         load_weights(0)
-        for i in range(LOAD_AHEAD):
-            load(i)
+        load(1)
         load_bias()
+        load(2)
         load_weights(1)
-        for k in range(-3, PAIRS + 2):
+        load(3)
+        transpose(0)
+        regroup(0)
+        transpose(1)
+        order_weights(0)
+        quantise_input(0)
+        quantise_weights(0)
+        project(0)
+        order_weights(1)
+        add_residual(0)
+        magnitude_share(0)
+        regroup(1)
+        transpose(2)
+        load(4)
+        quantise_input(1)
+        project(1)
+        for k in range(PAIRS):
             each(load, k + 3 + LOAD_AHEAD)
-            each(squash_factor, k)
+            each(squash_factor if k < LAST else squash_factor_last, k)
             each(squash_apply, k - 1)
             each(regroup, k + 2)
             each(transpose, k + 3)
@@ -257,9 +368,11 @@ def tile_decoder_pb_t_kernel(tc, hq1, hk1, proj1, bias1, out):
             each(store, k - 2)
             each(magnitude_share, k + 1)
             each(squash_apply_share, k - 1)
-            if 0 <= k + 2 < H:
-                quantise_weights(k + 2)
             each(quantise_input, k + 2)
             each(project, k + 2)
             each(quantise_hash, k - 1)
             each(scores, k - 1)
+            if k == 1:
+                quantise_weights(1)
+        store(LAST - 1)
+        finish(LAST)

@@ -23,7 +23,7 @@ ABS_SHARE = 96
 MUL_SHARE = 96
 LOAD_AHEAD = 2
 
-BY_CHUNK = 2
+EARLY, EARLY_SHARE = 8, 128
 LAST = PAIRS - 1
 
 FLOPS = 2 * PAIRS * (TOK * D * D + S * S * D)
@@ -121,7 +121,8 @@ def tile_decoder_pb_t_kernel(tc, hq1, hk1, proj1, bias1, out):
             x_t = work.tile([P, TOK * PACK], BF16, align_bytes=64)
             by_token = x_t[:].bitcast(F32).rearrange("p (s u) -> p s u", u=2)
             for side in range(2):
-                nc.vector.tensor_copy(
+                copy = nc.scalar.copy if 0 < i + side and i < 2 else nc.vector.tensor_copy
+                copy(
                     out=by_token[:, side * S : (side + 1) * S, :],
                     in_=tiles["xt", i, side][:].rearrange("p u s -> p s u"),
                 )
@@ -167,36 +168,40 @@ def tile_decoder_pb_t_kernel(tc, hq1, hk1, proj1, bias1, out):
                 )
             tiles["z", i] = z
 
+        def vector_share(i):
+            return 0 if i == 0 else EARLY_SHARE if i < EARLY else ABS_SHARE if i < LAST else S
+
+        def vector_magnitude(mag, z):
+            nc.vector.scalar_tensor_tensor(
+                out=mag, in0=z, scalar=-1.0, in1=z, op0=ALU.mult, op1=ALU.max
+            )
+
         def magnitude_share(i):
             mag_keys = work.tile([P, PACK, S], F32)
             tiles["mag_keys", i] = mag_keys
-            if i < BY_CHUNK:
-                return
-            share = S if i == LAST else ABS_SHARE
-            z_share = tiles["z", i][:, :, TOK - share :]
-            nc.vector.scalar_tensor_tensor(
-                out=mag_keys[:, :, S - share :],
-                in0=z_share,
-                scalar=-1.0,
-                in1=z_share,
-                op0=ALU.mult,
-                op1=ALU.max,
-            )
+            share = vector_share(i)
+            if share:
+                vector_magnitude(mag_keys[:, :, S - share :], tiles["z", i][:, :, TOK - share :])
+            if i == LAST:
+                mag_queries = work.tile([P, PACK, S], F32)
+                tiles["mag_queries", i] = mag_queries
+                vector_magnitude(mag_queries[:, :, P:], tiles["z", i][:, :, P:S])
 
         def squash_factor(i):
             z = tiles["z", i]
             r = work.tile([P, PACK, TOK], F32)
             mag_queries = work.tile([P, PACK, S], F32)
             mag_keys = tiles["mag_keys", i]
-            if i < BY_CHUNK:
+            share = vector_share(i)
+            if i == 0:
                 for c in range(PACK):
                     nc.scalar.activation(out=mag_queries[:, c, :], in_=z[:, c, :S], func=ACT.Abs)
                     nc.scalar.activation(out=mag_keys[:, c, :], in_=z[:, c, S:], func=ACT.Abs)
             else:
                 nc.scalar.activation(out=mag_queries[:], in_=z[:, :, :S], func=ACT.Abs)
                 nc.scalar.activation(
-                    out=mag_keys[:, :, : S - ABS_SHARE],
-                    in_=z[:, :, S : TOK - ABS_SHARE],
+                    out=mag_keys[:, :, : S - share],
+                    in_=z[:, :, S : TOK - share],
                     func=ACT.Abs,
                 )
             roots = []
@@ -221,8 +226,7 @@ def tile_decoder_pb_t_kernel(tc, hq1, hk1, proj1, bias1, out):
 
         def squash_factor_last(i):
             r = work.tile([P, PACK, TOK], F32)
-            mag_queries = work.tile([P, PACK, S], F32)
-            mag_keys = tiles["mag_keys", i]
+            mag_queries, mag_keys = tiles["mag_queries", i], tiles["mag_keys", i]
             root_q = work.tile([P, PACK, S], F32, tag="root")
             root_k = work.tile([P, PACK, S], F32, tag="root")
 
@@ -234,7 +238,9 @@ def tile_decoder_pb_t_kernel(tc, hq1, hk1, proj1, bias1, out):
             def factor(out, in_):
                 nc.scalar.activation(out=out, in_=in_, func=ACT.Square, scale=GAMMA**0.5)
 
-            nc.scalar.activation(out=mag_queries[:], in_=tiles["z", i][:, :, :S], func=ACT.Abs)
+            nc.scalar.activation(
+                out=mag_queries[:, :, :P], in_=tiles["z", i][:, :, :P], func=ACT.Abs
+            )
             root(root_k[:], mag_keys[:])
             root(root_q[:, :, :P], mag_queries[:, :, :P])
             factor(r[:, :, S:], root_k[:])
@@ -336,26 +342,26 @@ def tile_decoder_pb_t_kernel(tc, hq1, hk1, proj1, bias1, out):
             if 0 <= i < PAIRS:
                 stage(i)
 
-        load(0)
         load_weights(0)
+        load(0)
         load(1)
         load_bias()
         load(2)
         load_weights(1)
         load(3)
         transpose(0)
+        order_weights(0)
         regroup(0)
         transpose(1)
-        order_weights(0)
-        quantise_input(0)
         quantise_weights(0)
+        quantise_input(0)
         project(0)
-        order_weights(1)
-        add_residual(0)
-        magnitude_share(0)
         regroup(1)
         transpose(2)
+        order_weights(1)
         load(4)
+        add_residual(0)
+        magnitude_share(0)
         quantise_input(1)
         project(1)
         for k in range(PAIRS):

@@ -36,7 +36,8 @@ def tile_decoder_pb_t_kernel(tc, hq1, hk1, proj1, bias1, out):
         keep = ctx.enter_context(tc.tile_pool(name="keep", bufs=1))
         setup = ctx.enter_context(tc.tile_pool(name="setup", bufs=2))
         loads = ctx.enter_context(tc.tile_pool(name="loads", bufs=4))
-        work = ctx.enter_context(tc.tile_pool(name="work", bufs=2))
+        work = ctx.enter_context(tc.tile_pool(name="work", bufs=3))
+        results = ctx.enter_context(tc.tile_pool(name="results", bufs=PAIRS))
         sums = ctx.enter_context(tc.tile_pool(name="sums", bufs=3))
         psum_t = ctx.enter_context(tc.psum_pool(name="psum_t", bufs=2))
         psum_a = ctx.enter_context(tc.psum_pool(name="psum_a", bufs=4))
@@ -333,7 +334,7 @@ def tile_decoder_pb_t_kernel(tc, hq1, hk1, proj1, bias1, out):
 
         def store(i):
             h, b = divmod(i, B)
-            result = work.tile([P, S // P, S], F32)
+            result = results.tile([P, S // P, S], F32)
             copy = nc.vector.tensor_copy if i < LAST - 2 else nc.scalar.copy
             copy(out=result[:], in_=tiles["prod", i][:])
             nc.sync.dma_start(out=out[b, h].rearrange("(j m) k -> m j k", m=P), in_=result[:])

from contextlib import ExitStack

import concourse.mybir as mybir
from concourse.masks import make_identity

F32 = mybir.dt.float32
BF16 = mybir.dt.bfloat16
U32 = mybir.dt.uint32
U8 = mybir.dt.uint8
FP8X4 = mybir.dt.float8_e4m3fn_x4
ACT = mybir.ActivationFunctionType
ALU = mybir.AluOpType

P = 128
PACK = 4
B, H, S, D = 16, 2, 256, 512
PAIRS = B * H
TOK = 2 * S
WORDS = D // 2
GAMMA = 64.0
RUN = 4
ABS_SHARE = 96
MUL_SHARE = 96
LOAD_AHEAD = 2

EARLY, EARLY_SHARE = 8, 128
LAST = PAIRS - 1

FLOPS = 2 * PAIRS * (TOK * D * D + S * S * D)


def tile_decoder_pb_t_kernel(tc, hq1, hk1, proj1, bias1, out):
    nc = tc.nc
    with ExitStack() as ctx:
        ctx.enter_context(tc.manual_schedule())
        keep = ctx.enter_context(tc.tile_pool(name="keep", bufs=1))
        setup = ctx.enter_context(tc.tile_pool(name="setup", bufs=2))
        loads = ctx.enter_context(tc.tile_pool(name="loads", bufs=4))
        work = ctx.enter_context(tc.tile_pool(name="work", bufs=3))
        results = ctx.enter_context(tc.tile_pool(name="results", bufs=PAIRS))
        sums = ctx.enter_context(tc.tile_pool(name="sums", bufs=3))
        psum_t = ctx.enter_context(tc.psum_pool(name="psum_t", bufs=2))
        psum_a = ctx.enter_context(tc.psum_pool(name="psum_a", bufs=4))
        psum_o = ctx.enter_context(tc.psum_pool(name="psum_o", bufs=2))

        tiles = {}

        ident = keep.tile([P, P], F32)
        make_identity(nc, ident[:])
        one = keep.tile([P, 1], F32)
        nc.vector.memset(one[:], 1.0)
        warm = keep.tile([P, 1], F32)
        nc.scalar.activation(out=warm[:], in_=one[:], func=ACT.Abs_reciprocal_sqrt)

        bias = keep.tile([P, H * PACK], BF16)

        def load_bias():
            nc.sync.dma_start(
                out=bias[:].rearrange("p (a e) -> p a e", e=2),
                in_=bias1.rearrange("o h i (u p e) -> p (o h i u) e", u=2, e=2),
            )

        w_codes = keep.tile([P, H, D], U32, align_bytes=64)
        w_scales = keep.tile([P, H, D], U8, align_bytes=64)

        def load_weights(h):
            rows = setup.tile([P, PACK, D], BF16)
            nc.sync.dma_start(
                out=rows[:].rearrange("p (u e) n -> p u (e n)", e=2),
                in_=proj1[0, h].rearrange("(u p e) n -> p u (e n)", u=2, e=2),
            )
            tiles["rows", h] = rows

        def order_weights(h):
            by_chunk = tiles["rows", h][:].rearrange("p t (u m e) -> p u e m t", u=2, e=2)
            w_words = setup.tile([P, PACK, P, PACK], BF16, align_bytes=64)
            for c in range(PACK):
                chunk = by_chunk[:, c // 2, c % 2, :, :]
                if h == 1:
                    nc.gpsimd.tensor_scalar(
                        out=w_words[:, c, :, :],
                        in0=chunk,
                        scalar1=1.0,
                        scalar2=0.0,
                        op0=ALU.mult,
                        op1=ALU.add,
                    )
                else:
                    copy = nc.scalar.copy if c < PACK // 2 else nc.vector.tensor_copy
                    copy(out=w_words[:, c, :, :], in_=chunk)
            tiles["w_words", h] = w_words

        def quantise_weights(h):
            nc.vector.quantize_mx(
                out=w_codes[:, h, :].bitcast(FP8X4),
                scales=w_scales[:, h, :],
                in_=tiles["w_words", h][:].rearrange("p c m t -> p (c m t)"),
            )

        def load(i):
            h, b = divmod(i, B)
            x = loads.tile([P, 2, S // P, D], BF16)
            for side, src in enumerate((hq1, hk1)):
                nc.sync.dma_start(
                    out=x[:, side, :, :], in_=src[b, h].rearrange("(j p) d -> p j d", p=P)
                )
            tiles["x", i] = x

        def transpose(i):
            words = tiles["x", i][:].rearrange("p a j d -> p (a j d)").bitcast(F32)
            for side in range(2):
                xt = psum_t.tile([P, 2, S], F32)
                for j in range(S // P):
                    for u in range(2):
                        first = (side * (S // P) + j) * WORDS + u * P
                        nc.tensor.transpose(
                            xt[:, u, j * P : (j + 1) * P], words[:, first : first + P], ident[:]
                        )
                tiles["xt", i, side] = xt

        def regroup(i):
            x_t = work.tile([P, TOK * PACK], BF16, align_bytes=64)
            by_token = x_t[:].bitcast(F32).rearrange("p (s u) -> p s u", u=2)
            for side in range(2):
                copy = nc.scalar.copy if 0 < i + side and i < 2 else nc.vector.tensor_copy
                copy(
                    out=by_token[:, side * S : (side + 1) * S, :],
                    in_=tiles["xt", i, side][:].rearrange("p u s -> p s u"),
                )
            tiles["x_t", i] = x_t

        def quantise_input(i):
            x_codes = work.tile([P, TOK], U32, align_bytes=64)
            x_scales = work.tile([P, TOK], U8, align_bytes=64)
            nc.vector.quantize_mx(
                out=x_codes[:].bitcast(FP8X4), scales=x_scales[:], in_=tiles["x_t", i][:]
            )
            tiles["x_mx", i] = (x_codes, x_scales)

        def project(i):
            h = i // B
            x_codes, x_scales = tiles["x_mx", i]
            for c in range(PACK):
                cols = slice(c * P, (c + 1) * P)
                acc = psum_a.tile([P, TOK], F32)
                nc.tensor.matmul_mx(
                    out=acc[:],
                    lhsT=w_codes[:, h, cols].bitcast(FP8X4),
                    lhsT_scale=w_scales[:, h, cols],
                    rhs=x_codes[:].bitcast(FP8X4),
                    rhs_scale=x_scales[:],
                    start=True,
                    stop=True,
                )
                tiles["acc", i, c] = acc

        def add_residual(i):
            h = i // B
            residual = tiles["x_t", i][:].rearrange("p (s t) -> p s t", t=PACK)
            z = sums.tile([P, PACK, TOK], F32)
            for c in range(PACK):
                nc.vector.scalar_tensor_tensor(
                    out=z[:, c, :],
                    in0=tiles["acc", i, c][:],
                    scalar=bias[:, h * PACK + c : h * PACK + c + 1],
                    in1=residual[:, :, c],
                    op0=ALU.add,
                    op1=ALU.add,
                )
            tiles["z", i] = z

        def vector_share(i):
            return 0 if i == 0 else EARLY_SHARE if i < EARLY else ABS_SHARE if i < LAST else S

        def vector_magnitude(mag, z):
            nc.vector.scalar_tensor_tensor(
                out=mag, in0=z, scalar=-1.0, in1=z, op0=ALU.mult, op1=ALU.max
            )

        def magnitude_share(i):
            mag_keys = work.tile([P, PACK, S], F32)
            tiles["mag_keys", i] = mag_keys
            share = vector_share(i)
            if share:
                vector_magnitude(mag_keys[:, :, S - share :], tiles["z", i][:, :, TOK - share :])
            if i == LAST:
                mag_queries = work.tile([P, PACK, S], F32)
                tiles["mag_queries", i] = mag_queries
                vector_magnitude(mag_queries[:, :, P:], tiles["z", i][:, :, P:S])

        def squash_factor(i):
            z = tiles["z", i]
            r = work.tile([P, PACK, TOK], F32)
            mag_queries = work.tile([P, PACK, S], F32)
            mag_keys = tiles["mag_keys", i]
            share = vector_share(i)
            if i == 0:
                for c in range(PACK):
                    nc.scalar.activation(out=mag_queries[:, c, :], in_=z[:, c, :S], func=ACT.Abs)
                    nc.scalar.activation(out=mag_keys[:, c, :], in_=z[:, c, S:], func=ACT.Abs)
            else:
                nc.scalar.activation(out=mag_queries[:], in_=z[:, :, :S], func=ACT.Abs)
                nc.scalar.activation(
                    out=mag_keys[:, :, : S - share],
                    in_=z[:, :, S : TOK - share],
                    func=ACT.Abs,
                )
            roots = []
            for mag in (mag_queries, mag_keys):
                root = work.tile([P, PACK, S], F32)
                nc.scalar.activation(
                    out=root[:],
                    in_=mag[:],
                    func=ACT.Abs_reciprocal_sqrt,
                    scale=GAMMA,
                    bias=one[:, 0:1],
                )
                roots.append(root)
            for side, root in enumerate(roots):
                nc.scalar.activation(
                    out=r[:, :, side * S : (side + 1) * S],
                    in_=root[:],
                    func=ACT.Square,
                    scale=GAMMA**0.5,
                )
            tiles["r", i] = r

        def squash_factor_last(i):
            r = work.tile([P, PACK, TOK], F32)
            mag_queries, mag_keys = tiles["mag_queries", i], tiles["mag_keys", i]
            root_q = work.tile([P, PACK, S], F32, tag="root")
            root_k = work.tile([P, PACK, S], F32, tag="root")

            def root(out, in_):
                nc.scalar.activation(
                    out=out, in_=in_, func=ACT.Abs_reciprocal_sqrt, scale=GAMMA, bias=one[:, 0:1]
                )

            def factor(out, in_):
                nc.scalar.activation(out=out, in_=in_, func=ACT.Square, scale=GAMMA**0.5)

            nc.scalar.activation(
                out=mag_queries[:, :, :P], in_=tiles["z", i][:, :, :P], func=ACT.Abs
            )
            root(root_k[:], mag_keys[:])
            root(root_q[:, :, :P], mag_queries[:, :, :P])
            factor(r[:, :, S:], root_k[:])
            root(root_q[:, :, P:], mag_queries[:, :, P:])
            factor(r[:, :, :P], root_q[:, :, :P])
            factor(r[:, :, P:S], root_q[:, :, P:])
            tiles["r", i] = r

        def multiply(engine, i, tokens):
            by_token = tiles["y", i][:].rearrange("p (s t) -> p s t", t=PACK)
            engine.tensor_tensor(
                out=by_token[:, tokens, :].rearrange("p (n i) t -> p n t i", i=RUN),
                in0=tiles["z", i][:, :, tokens].rearrange("p t (n i) -> p n t i", i=RUN),
                in1=tiles["r", i][:, :, tokens].rearrange("p t (n i) -> p n t i", i=RUN),
                op=ALU.mult,
            )

        def squash_apply(i):
            y = work.tile([P, TOK * PACK], BF16, align_bytes=64)
            tiles["y", i] = y
            if i >= LAST - 1:
                return
            multiply(nc.gpsimd, i, slice(S, TOK - MUL_SHARE))
            multiply(nc.gpsimd, i, slice(0, S))

        def squash_apply_share(i):
            multiply(nc.vector, i, slice(TOK - MUL_SHARE if i < LAST - 1 else 0, TOK))

        def quantise_hash(i):
            y_codes = work.tile([P, TOK], U32, align_bytes=64)
            y_scales = work.tile([P, TOK], U8, align_bytes=64)
            nc.vector.quantize_mx(
                out=y_codes[:].bitcast(FP8X4), scales=y_scales[:], in_=tiles["y", i][:]
            )
            tiles["y_mx", i] = (y_codes, y_scales)

        def finish(i):
            h, b = divmod(i, B)
            y = work.tile([P, TOK * PACK], BF16, align_bytes=64)
            tiles["y", i] = y
            y_codes = work.tile([P, TOK], U32, align_bytes=64)
            y_scales = work.tile([P, TOK], U8, align_bytes=64)
            keys, halves = slice(S, TOK), (slice(0, P), slice(P, S))

            def quantise(tokens):
                nc.vector.quantize_mx(
                    out=y_codes[:, tokens].bitcast(FP8X4),
                    scales=y_scales[:, tokens],
                    in_=y[:, tokens.start * PACK : tokens.stop * PACK],
                )

            multiply(nc.vector, i, keys)
            multiply(nc.vector, i, halves[0])
            quantise(keys)
            quantise(halves[0])
            multiply(nc.vector, i, halves[1])
            quantise(halves[1])
            for j, queries in enumerate(halves):
                acc = psum_a.tile([P, TOK], F32)
                nc.tensor.matmul_mx(
                    out=acc[:, :S],
                    lhsT=y_codes[:, queries].bitcast(FP8X4),
                    lhsT_scale=y_scales[:, queries],
                    rhs=y_codes[:, keys].bitcast(FP8X4),
                    rhs_scale=y_scales[:, keys],
                    start=True,
                    stop=True,
                )
                half = work.tile([P, S], F32)
                copy = nc.scalar.copy if j == 0 else nc.vector.tensor_copy
                copy(out=half[:], in_=acc[:, :S])
                nc.sync.dma_start(out=out[b, h, queries, :], in_=half[:])

        def scores(i):
            y_codes, y_scales = tiles["y_mx", i]
            keys = slice(S, TOK)
            prod = psum_o.tile([P, S // P, S], F32)
            for j in range(S // P):
                queries = slice(j * P, (j + 1) * P)
                nc.tensor.matmul_mx(
                    out=prod[:, j, :],
                    lhsT=y_codes[:, queries].bitcast(FP8X4),
                    lhsT_scale=y_scales[:, queries],
                    rhs=y_codes[:, keys].bitcast(FP8X4),
                    rhs_scale=y_scales[:, keys],
                    start=True,
                    stop=True,
                )
            tiles["prod", i] = prod

        def store(i):
            h, b = divmod(i, B)
            result = results.tile([P, S // P, S], F32)
            copy = nc.vector.tensor_copy if i < LAST - 2 else nc.scalar.copy
            copy(out=result[:], in_=tiles["prod", i][:])
            nc.sync.dma_start(out=out[b, h].rearrange("(j m) k -> m j k", m=P), in_=result[:])

        def each(stage, i):
            if 0 <= i < PAIRS:
                stage(i)

        load_weights(0)
        load(0)
        load(1)
        load_bias()
        load(2)
        load_weights(1)
        load(3)
        transpose(0)
        order_weights(0)
        regroup(0)
        transpose(1)
        quantise_weights(0)
        quantise_input(0)
        project(0)
        regroup(1)
        transpose(2)
        order_weights(1)
        load(4)
        add_residual(0)
        magnitude_share(0)
        quantise_input(1)
        project(1)
        for k in range(PAIRS):
            each(load, k + 3 + LOAD_AHEAD)
            each(squash_factor if k < LAST else squash_factor_last, k)
            each(squash_apply, k - 1)
            each(regroup, k + 2)
            each(transpose, k + 3)
            each(add_residual, k + 1)
            each(store, k - 2)
            each(magnitude_share, k + 1)
            each(squash_apply_share, k - 1)
            each(quantise_input, k + 2)
            each(project, k + 2)
            each(quantise_hash, k - 1)
            each(scores, k - 1)
            if k == 1:
                quantise_weights(1)
        store(LAST - 1)
        finish(LAST)
